import numpy as np
import ml_dtypes

BF16 = ml_dtypes.bfloat16


def bf(x):
    return np.asarray(x, np.float32).astype(BF16)


def f32(x):
    return np.asarray(x, np.float32)


def f64(x):
    return np.asarray(x).astype(np.float64)


def striped(idx):
    return np.tile(idx.reshape(-1, 16).T, (8, 1))


F, P, D, C, S, K, H, N = 128, 5, 3, 768, 256, 8, 128, 1024


def setup_inputs():
    x0 = f32(0.7 * np.random.standard_normal((F, N)))
    x1 = f32(0.7 * np.random.standard_normal((D * F, N)))
    wt = f32(np.random.standard_normal((C, S)))
    idx = np.concatenate([np.random.permutation(S)[:H] for _ in range(K)])
    return {"x0": x0, "x1": x1, "wt": wt, "offs": striped(idx)}


def reference(x0, x1, wt, offs):
    idx = offs[:16].T.reshape(-1)
    a = f64(x0)
    v = f64(x1).reshape(D, F, N)
    dot = (v * v).sum(axis=0)
    w = f64(wt)[:, idx].reshape(-1, F, N)
    paths = np.stack([a, a * a, dot, a * a * a, a * dot], axis=0)
    contracted = (paths * w[:P]).sum(axis=0)
    return contracted * w[P]

@@ -1,0 +1,61 @@
+import concourse.mybir as mybir
+
+F32 = mybir.dt.float32
+U16 = mybir.dt.uint16
+MULT = mybir.AluOpType.mult
+ADD = mybir.AluOpType.add
+SQUARE = mybir.ActivationFunctionType.Square
+
+FEATURES = 128
+NODES = 1024
+SPECIES = 256
+PATHS = 5
+DIMS = 3
+PIECE = 256
+PIECE_OFFSET_COLUMNS = PIECE // 16
+
+
+def tile_equivariantproductbasisblock_kernel(tc, x0, x1, wt, offs, out):
+    nc = tc.nc
+    with (
+        tc.tile_pool(name="held", bufs=1) as held,
+        tc.tile_pool(name="work", bufs=2) as work,
+    ):
+        offsets = held.tile([FEATURES, NODES // 16], U16, name="offsets")
+        nc.sync.dma_start(offsets[:], offs)
+        tables = [held.tile([FEATURES, SPECIES], F32, name=f"table{b}") for b in range(PATHS + 1)]
+        scalars = held.tile([FEATURES, NODES], F32, name="scalars")
+        nc.sync.dma_start(tables[0][:], wt[0:FEATURES, :])
+        nc.sync.dma_start(scalars[:], x0)
+        vectors = [held.tile([FEATURES, NODES], F32, name=f"vectors{d}") for d in range(DIMS)]
+        for d in range(DIMS):
+            nc.scalar.dma_start(vectors[d][:], x1[d * FEATURES : (d + 1) * FEATURES, :])
+        for b in range(1, PATHS + 1):
+            nc.sync.dma_start(tables[b][:], wt[b * FEATURES : (b + 1) * FEATURES, :])
+
+        square = held.tile([FEATURES, NODES], F32, name="square")
+        nc.scalar.activation(square[:], scalars[:], SQUARE)
+        squares = [held.tile([FEATURES, NODES], F32, name=f"squares{d}") for d in range(DIMS)]
+        for d in range(DIMS):
+            nc.scalar.activation(squares[d][:], vectors[d][:], SQUARE)
+        cube = held.tile([FEATURES, NODES], F32, name="cube")
+        nc.vector.tensor_tensor(cube[:], square[:], scalars[:], MULT)
+        dot = held.tile([FEATURES, NODES], F32, name="dot")
+        nc.vector.tensor_tensor(dot[:], squares[0][:], squares[1][:], ADD)
+        nc.vector.tensor_tensor(dot[:], dot[:], squares[2][:], ADD)
+        scalar_dot = held.tile([FEATURES, NODES], F32, name="scalar_dot")
+        nc.vector.tensor_tensor(scalar_dot[:], scalars[:], dot[:], MULT)
+        paths = [scalars, square, dot, cube, scalar_dot]
+
+        for k in range(NODES // PIECE):
+            nodes = slice(k * PIECE, (k + 1) * PIECE)
+            piece = offsets[:, k * PIECE_OFFSET_COLUMNS : (k + 1) * PIECE_OFFSET_COLUMNS]
+            contracted = work.tile([FEATURES, PIECE], F32, name="contracted")
+            nc.vector.tensor_tensor(contracted[:], tables[0][:].indirect(piece), paths[0][:, nodes], MULT)
+            for p in range(1, PATHS):
+                product = work.tile([FEATURES, PIECE], F32, name="product")
+                nc.vector.tensor_tensor(product[:], tables[p][:].indirect(piece), paths[p][:, nodes], MULT)
+                nc.vector.tensor_tensor(contracted[:], contracted[:], product[:], ADD)
+            gated = work.tile([FEATURES, PIECE], F32, name="gated")
+            nc.vector.tensor_tensor(gated[:], tables[PATHS][:].indirect(piece), contracted[:], MULT)
+            nc.sync.dma_start(out[:, nodes], gated[:])

@@ -1,10 +1,12 @@
 import concourse.mybir as mybir
+from concourse.masks import make_identity
 
 F32 = mybir.dt.float32
 U16 = mybir.dt.uint16
 MULT = mybir.AluOpType.mult
 ADD = mybir.AluOpType.add
 SQUARE = mybir.ActivationFunctionType.Square
+COPY = mybir.ActivationFunctionType.Copy
 
 FEATURES = 128
 NODES = 1024
@@ -12,50 +14,77 @@ SPECIES = 256
 PATHS = 5
 DIMS = 3
 PIECE = 256
+PIECES = NODES // PIECE
 PIECE_OFFSET_COLUMNS = PIECE // 16
+PATH_ORDER = (0, 1, 3, 2, 4)
 
 
 def tile_equivariantproductbasisblock_kernel(tc, x0, x1, wt, offs, out):
     nc = tc.nc
+
+    def nodes(k):
+        return slice(k * PIECE, (k + 1) * PIECE)
+
     with (
         tc.tile_pool(name="held", bufs=1) as held,
-        tc.tile_pool(name="work", bufs=2) as work,
+        tc.psum_pool(name="banks", bufs=1) as banks,
     ):
         offsets = held.tile([FEATURES, NODES // 16], U16, name="offsets")
         nc.sync.dma_start(offsets[:], offs)
+
+        def looked_up(table, k):
+            return table[:].indirect(offsets[:, k * PIECE_OFFSET_COLUMNS : (k + 1) * PIECE_OFFSET_COLUMNS])
+
         tables = [held.tile([FEATURES, SPECIES], F32, name=f"table{b}") for b in range(PATHS + 1)]
         scalars = held.tile([FEATURES, NODES], F32, name="scalars")
-        nc.sync.dma_start(tables[0][:], wt[0:FEATURES, :])
-        nc.sync.dma_start(scalars[:], x0)
         vectors = [held.tile([FEATURES, NODES], F32, name=f"vectors{d}") for d in range(DIMS)]
-        for d in range(DIMS):
-            nc.scalar.dma_start(vectors[d][:], x1[d * FEATURES : (d + 1) * FEATURES, :])
-        for b in range(1, PATHS + 1):
-            nc.sync.dma_start(tables[b][:], wt[b * FEATURES : (b + 1) * FEATURES, :])
+
+        def table_load(b):
+            return (tables[b][:], wt[b * FEATURES : (b + 1) * FEATURES, :])
+
+        loads = [table_load(0)]
+        loads += [(scalars[:, nodes(k)], x0[:, nodes(k)]) for k in range(PIECES)]
+        loads += [table_load(1), table_load(3)]
+        loads += [(vectors[d][:], x1[d * FEATURES : (d + 1) * FEATURES, :]) for d in range(DIMS)]
+        loads += [table_load(2), table_load(4), table_load(PATHS)]
+        for i, (tile_side, dram_side) in enumerate(loads):
+            queue = nc.scalar if i % 2 == 0 else nc.sync
+            queue.dma_start(tile_side, dram_side)
+
+        identity = held.tile([FEATURES, FEATURES], F32, name="identity")
+        make_identity(nc, identity[:])
 
         square = held.tile([FEATURES, NODES], F32, name="square")
-        nc.scalar.activation(square[:], scalars[:], SQUARE)
+        for k in range(PIECES):
+            nc.scalar.activation(square[:, nodes(k)], scalars[:, nodes(k)], SQUARE)
         squares = [held.tile([FEATURES, NODES], F32, name=f"squares{d}") for d in range(DIMS)]
         for d in range(DIMS):
             nc.scalar.activation(squares[d][:], vectors[d][:], SQUARE)
-        cube = held.tile([FEATURES, NODES], F32, name="cube")
-        nc.vector.tensor_tensor(cube[:], square[:], scalars[:], MULT)
-        dot = held.tile([FEATURES, NODES], F32, name="dot")
-        nc.vector.tensor_tensor(dot[:], squares[0][:], squares[1][:], ADD)
-        nc.vector.tensor_tensor(dot[:], dot[:], squares[2][:], ADD)
-        scalar_dot = held.tile([FEATURES, NODES], F32, name="scalar_dot")
-        nc.vector.tensor_tensor(scalar_dot[:], scalars[:], dot[:], MULT)
-        paths = [scalars, square, dot, cube, scalar_dot]
 
-        for k in range(NODES // PIECE):
-            nodes = slice(k * PIECE, (k + 1) * PIECE)
-            piece = offsets[:, k * PIECE_OFFSET_COLUMNS : (k + 1) * PIECE_OFFSET_COLUMNS]
-            contracted = work.tile([FEATURES, PIECE], F32, name="contracted")
-            nc.vector.tensor_tensor(contracted[:], tables[0][:].indirect(piece), paths[0][:, nodes], MULT)
-            for p in range(1, PATHS):
-                product = work.tile([FEATURES, PIECE], F32, name="product")
-                nc.vector.tensor_tensor(product[:], tables[p][:].indirect(piece), paths[p][:, nodes], MULT)
-                nc.vector.tensor_tensor(contracted[:], contracted[:], product[:], ADD)
-            gated = work.tile([FEATURES, PIECE], F32, name="gated")
-            nc.vector.tensor_tensor(gated[:], tables[PATHS][:].indirect(piece), contracted[:], MULT)
-            nc.sync.dma_start(out[:, nodes], gated[:])
+        cube = held.tile([FEATURES, NODES], F32, name="cube")
+        dot = held.tile([FEATURES, NODES], F32, name="dot")
+        scalar_dot = held.tile([FEATURES, NODES], F32, name="scalar_dot")
+        paths = [scalars, square, dot, cube, scalar_dot]
+        products = [held.tile([FEATURES, NODES], F32, name=f"products{p}") for p in range(PATHS)]
+        sums = [banks.tile([FEATURES, PIECE], F32, name=f"sums{k}") for k in range(PIECES)]
+
+        for p in PATH_ORDER:
+            if p == 3:
+                nc.vector.tensor_tensor(cube[:], square[:], scalars[:], MULT)
+            if p == 2:
+                nc.vector.tensor_tensor(dot[:], squares[0][:], squares[1][:], ADD)
+                nc.vector.tensor_tensor(dot[:], dot[:], squares[2][:], ADD)
+            if p == 4:
+                nc.vector.tensor_tensor(scalar_dot[:], scalars[:], dot[:], MULT)
+            for k in range(PIECES):
+                nc.vector.tensor_tensor(products[p][:, nodes(k)], looked_up(tables[p], k), paths[p][:, nodes(k)], MULT)
+                nc.tensor.matmul(
+                    sums[k][:], identity[:], products[p][:, nodes(k)], start=p == PATH_ORDER[0], stop=p == PATH_ORDER[-1]
+                )
+
+        contracted = held.tile([FEATURES, NODES], F32, name="contracted")
+        gated = held.tile([FEATURES, NODES], F32, name="gated")
+        for k in range(PIECES):
+            nc.scalar.activation(contracted[:, nodes(k)], sums[k][:], COPY)
+            nc.vector.tensor_tensor(gated[:, nodes(k)], looked_up(tables[PATHS], k), contracted[:, nodes(k)], MULT)
+            nc.sync.dma_start(out[:, nodes(k)], gated[:, nodes(k)])

@@ -70,7 +70,8 @@ def tile_equivariantproductbasisblock_kernel(tc, x0, x1, wt, offs, out):
 
         for p in PATH_ORDER:
             if p == 3:
-                nc.vector.tensor_tensor(cube[:], square[:], scalars[:], MULT)
+                for k in range(PIECES):
+                    nc.gpsimd.tensor_tensor(cube[:, nodes(k)], square[:, nodes(k)], scalars[:, nodes(k)], MULT)
             if p == 2:
                 nc.vector.tensor_tensor(dot[:], squares[0][:], squares[1][:], ADD)
                 nc.vector.tensor_tensor(dot[:], dot[:], squares[2][:], ADD)

@@ -16,7 +16,8 @@ DIMS = 3
 PIECE = 256
 PIECES = NODES // PIECE
 PIECE_OFFSET_COLUMNS = PIECE // 16
-PATH_ORDER = (0, 1, 3, 2, 4)
+HALVES = (slice(0, NODES // 2), slice(NODES // 2, NODES))
+FIRST_PATH, LAST_PATH = 0, 4
 
 
 def tile_equivariantproductbasisblock_kernel(tc, x0, x1, wt, offs, out):
@@ -32,24 +33,21 @@ def tile_equivariantproductbasisblock_kernel(tc, x0, x1, wt, offs, out):
         offsets = held.tile([FEATURES, NODES // 16], U16, name="offsets")
         nc.sync.dma_start(offsets[:], offs)
 
-        def looked_up(table, k):
-            return table[:].indirect(offsets[:, k * PIECE_OFFSET_COLUMNS : (k + 1) * PIECE_OFFSET_COLUMNS])
-
         tables = [held.tile([FEATURES, SPECIES], F32, name=f"table{b}") for b in range(PATHS + 1)]
         scalars = held.tile([FEATURES, NODES], F32, name="scalars")
         vectors = [held.tile([FEATURES, NODES], F32, name=f"vectors{d}") for d in range(DIMS)]
 
-        def table_load(b):
-            return (tables[b][:], wt[b * FEATURES : (b + 1) * FEATURES, :])
+        def load_table(queue, b):
+            queue.dma_start(tables[b][:], wt[b * FEATURES : (b + 1) * FEATURES, :])
 
-        loads = [table_load(0)]
-        loads += [(scalars[:, nodes(k)], x0[:, nodes(k)]) for k in range(PIECES)]
-        loads += [table_load(1), table_load(3)]
-        loads += [(vectors[d][:], x1[d * FEATURES : (d + 1) * FEATURES, :]) for d in range(DIMS)]
-        loads += [table_load(2), table_load(4), table_load(PATHS)]
-        for i, (tile_side, dram_side) in enumerate(loads):
-            queue = nc.scalar if i % 2 == 0 else nc.sync
-            queue.dma_start(tile_side, dram_side)
+        load_table(nc.scalar, 0)
+        for k in range(PIECES):
+            nc.sync.dma_start(scalars[:, nodes(k)], x0[:, nodes(k)])
+        load_table(nc.sync, 1)
+        for d in range(DIMS):
+            nc.sync.dma_start(vectors[d][:], x1[d * FEATURES : (d + 1) * FEATURES, :])
+        for b in (3, 2, 4, PATHS):
+            load_table(nc.sync, b)
 
         identity = held.tile([FEATURES, FEATURES], F32, name="identity")
         make_identity(nc, identity[:])
@@ -68,24 +66,31 @@ def tile_equivariantproductbasisblock_kernel(tc, x0, x1, wt, offs, out):
         products = [held.tile([FEATURES, NODES], F32, name=f"products{p}") for p in range(PATHS)]
         sums = [banks.tile([FEATURES, PIECE], F32, name=f"sums{k}") for k in range(PIECES)]
 
-        for p in PATH_ORDER:
-            if p == 3:
-                for k in range(PIECES):
-                    nc.gpsimd.tensor_tensor(cube[:, nodes(k)], square[:, nodes(k)], scalars[:, nodes(k)], MULT)
-            if p == 2:
-                nc.vector.tensor_tensor(dot[:], squares[0][:], squares[1][:], ADD)
-                nc.vector.tensor_tensor(dot[:], dot[:], squares[2][:], ADD)
-            if p == 4:
-                nc.vector.tensor_tensor(scalar_dot[:], scalars[:], dot[:], MULT)
+        def looked_up(b, k):
+            return tables[b][:].indirect(offsets[:, k * PIECE_OFFSET_COLUMNS : (k + 1) * PIECE_OFFSET_COLUMNS])
+
+        def contract(p):
             for k in range(PIECES):
-                nc.vector.tensor_tensor(products[p][:, nodes(k)], looked_up(tables[p], k), paths[p][:, nodes(k)], MULT)
+                nc.vector.tensor_tensor(products[p][:, nodes(k)], looked_up(p, k), paths[p][:, nodes(k)], MULT)
                 nc.tensor.matmul(
-                    sums[k][:], identity[:], products[p][:, nodes(k)], start=p == PATH_ORDER[0], stop=p == PATH_ORDER[-1]
+                    sums[k][:], identity[:], products[p][:, nodes(k)], start=p == FIRST_PATH, stop=p == LAST_PATH
                 )
+
+        contract(0)
+        nc.vector.tensor_tensor(cube[:], square[:], scalars[:], MULT)
+        contract(1)
+        nc.vector.tensor_tensor(dot[:], squares[0][:], squares[1][:], ADD)
+        contract(3)
+        for half in HALVES:
+            nc.vector.tensor_tensor(dot[:, half], dot[:, half], squares[2][:, half], ADD)
+        contract(2)
+        for half in HALVES:
+            nc.vector.tensor_tensor(scalar_dot[:, half], scalars[:, half], dot[:, half], MULT)
+        contract(4)
 
         contracted = held.tile([FEATURES, NODES], F32, name="contracted")
         gated = held.tile([FEATURES, NODES], F32, name="gated")
         for k in range(PIECES):
             nc.scalar.activation(contracted[:, nodes(k)], sums[k][:], COPY)
-            nc.vector.tensor_tensor(gated[:, nodes(k)], looked_up(tables[PATHS], k), contracted[:, nodes(k)], MULT)
+            nc.vector.tensor_tensor(gated[:, nodes(k)], looked_up(PATHS, k), contracted[:, nodes(k)], MULT)
             nc.sync.dma_start(out[:, nodes(k)], gated[:, nodes(k)])

@@ -4,7 +4,6 @@ from concourse.masks import make_identity
 F32 = mybir.dt.float32
 U16 = mybir.dt.uint16
 MULT = mybir.AluOpType.mult
-ADD = mybir.AluOpType.add
 SQUARE = mybir.ActivationFunctionType.Square
 COPY = mybir.ActivationFunctionType.Copy
 
@@ -16,19 +15,25 @@ DIMS = 3
 PIECE = 256
 PIECES = NODES // PIECE
 PIECE_OFFSET_COLUMNS = PIECE // 16
-HALVES = (slice(0, NODES // 2), slice(NODES // 2, NODES))
+HALF = NODES // 2
+BLOCK = 128
 FIRST_PATH, LAST_PATH = 0, 4
 
 
 def tile_equivariantproductbasisblock_kernel(tc, x0, x1, wt, offs, out):
     nc = tc.nc
 
-    def nodes(k):
+    def piece(k):
         return slice(k * PIECE, (k + 1) * PIECE)
+
+    def half(h):
+        return slice(h * HALF, (h + 1) * HALF)
 
     with (
         tc.tile_pool(name="held", bufs=1) as held,
-        tc.psum_pool(name="banks", bufs=1) as banks,
+        tc.tile_pool(name="work", bufs=2) as work,
+        tc.psum_pool(name="sum_banks", bufs=1) as sum_banks,
+        tc.psum_pool(name="turn_banks", bufs=3) as turn_banks,
     ):
         offsets = held.tile([FEATURES, NODES // 16], U16, name="offsets")
         nc.sync.dma_start(offsets[:], offs)
@@ -40,57 +45,96 @@ def tile_equivariantproductbasisblock_kernel(tc, x0, x1, wt, offs, out):
         def load_table(queue, b):
             queue.dma_start(tables[b][:], wt[b * FEATURES : (b + 1) * FEATURES, :])
 
+        def load_vectors(h):
+            for d in range(DIMS):
+                nc.sync.dma_start(vectors[d][:, half(h)], x1[d * FEATURES : (d + 1) * FEATURES, half(h)])
+
         load_table(nc.scalar, 0)
         for k in range(PIECES):
-            nc.sync.dma_start(scalars[:, nodes(k)], x0[:, nodes(k)])
+            nc.sync.dma_start(scalars[:, piece(k)], x0[:, piece(k)])
         load_table(nc.sync, 1)
-        for d in range(DIMS):
-            nc.sync.dma_start(vectors[d][:], x1[d * FEATURES : (d + 1) * FEATURES, :])
-        for b in (3, 2, 4, PATHS):
+        load_vectors(0)
+        load_table(nc.sync, 3)
+        load_vectors(1)
+        for b in (2, 4, PATHS):
             load_table(nc.sync, b)
 
         identity = held.tile([FEATURES, FEATURES], F32, name="identity")
         make_identity(nc, identity[:])
 
-        square = held.tile([FEATURES, NODES], F32, name="square")
-        for k in range(PIECES):
-            nc.scalar.activation(square[:, nodes(k)], scalars[:, nodes(k)], SQUARE)
-        squares = [held.tile([FEATURES, NODES], F32, name=f"squares{d}") for d in range(DIMS)]
-        for d in range(DIMS):
-            nc.scalar.activation(squares[d][:], vectors[d][:], SQUARE)
+        def flip_onto(bank, tile, first_column, first, last):
+            blocks = bank.shape[1] // BLOCK
+            for b in range(blocks):
+                nc.tensor.matmul(
+                    bank[:, b * BLOCK : (b + 1) * BLOCK],
+                    tile[:, first_column + b * BLOCK : first_column + (b + 1) * BLOCK],
+                    identity[:],
+                    is_transpose=True,
+                    start=first and b == 0,
+                    stop=last and b == blocks - 1,
+                )
 
+        def flip_back(flipped_bank, first_column):
+            flipped = work.tile([BLOCK, PIECE], F32, name="flipped")
+            nc.scalar.activation(flipped[:], flipped_bank[:, first_column : first_column + PIECE], COPY)
+            upright_bank = turn_banks.tile([FEATURES, PIECE], F32, name="upright_bank", tag="turn")
+            flip_onto(upright_bank, flipped, 0, True, True)
+            return upright_bank
+
+        def copy_out(tile, k, upright_bank):
+            nc.scalar.activation(tile[:, piece(k)], upright_bank[:], COPY)
+
+        square = held.tile([FEATURES, NODES], F32, name="square")
+        squares = [held.tile([FEATURES, NODES], F32, name=f"squares{d}") for d in range(DIMS)]
         cube = held.tile([FEATURES, NODES], F32, name="cube")
         dot = held.tile([FEATURES, NODES], F32, name="dot")
         scalar_dot = held.tile([FEATURES, NODES], F32, name="scalar_dot")
         paths = [scalars, square, dot, cube, scalar_dot]
         products = [held.tile([FEATURES, NODES], F32, name=f"products{p}") for p in range(PATHS)]
-        sums = [banks.tile([FEATURES, PIECE], F32, name=f"sums{k}") for k in range(PIECES)]
+        flipped_sums = [sum_banks.tile([BLOCK, PIECE], F32, name=f"flipped_sums{k}") for k in range(PIECES)]
 
         def looked_up(b, k):
             return tables[b][:].indirect(offsets[:, k * PIECE_OFFSET_COLUMNS : (k + 1) * PIECE_OFFSET_COLUMNS])
 
+        def multiply(p, k):
+            nc.vector.tensor_tensor(products[p][:, piece(k)], looked_up(p, k), paths[p][:, piece(k)], MULT)
+            flip_onto(flipped_sums[k], products[p], k * PIECE, p == FIRST_PATH, p == LAST_PATH)
+
         def contract(p):
             for k in range(PIECES):
-                nc.vector.tensor_tensor(products[p][:, nodes(k)], looked_up(p, k), paths[p][:, nodes(k)], MULT)
-                nc.tensor.matmul(
-                    sums[k][:], identity[:], products[p][:, nodes(k)], start=p == FIRST_PATH, stop=p == LAST_PATH
-                )
+                multiply(p, k)
 
+        def make_dot(h):
+            flipped_dot = turn_banks.tile([BLOCK, HALF], F32, name="flipped_dot", tag="turn")
+            for d in range(DIMS):
+                nc.scalar.activation(squares[d][:, half(h)], vectors[d][:, half(h)], SQUARE)
+                flip_onto(flipped_dot, squares[d], h * HALF, d == 0, d == DIMS - 1)
+            upright_banks = [flip_back(flipped_dot, i * PIECE) for i in range(HALF // PIECE)]
+            for i in range(HALF // PIECE):
+                copy_out(dot, h * (HALF // PIECE) + i, upright_banks[i])
+
+        for k in range(PIECES):
+            nc.scalar.activation(square[:, piece(k)], scalars[:, piece(k)], SQUARE)
         contract(0)
         nc.vector.tensor_tensor(cube[:], square[:], scalars[:], MULT)
+        make_dot(0)
         contract(1)
-        nc.vector.tensor_tensor(dot[:], squares[0][:], squares[1][:], ADD)
+        make_dot(1)
         contract(3)
-        for half in HALVES:
-            nc.vector.tensor_tensor(dot[:, half], dot[:, half], squares[2][:, half], ADD)
         contract(2)
-        for half in HALVES:
-            nc.vector.tensor_tensor(scalar_dot[:, half], scalars[:, half], dot[:, half], MULT)
-        contract(4)
+        for h in range(NODES // HALF):
+            nc.vector.tensor_tensor(scalar_dot[:, half(h)], scalars[:, half(h)], dot[:, half(h)], MULT)
 
         contracted = held.tile([FEATURES, NODES], F32, name="contracted")
+        upright_sums = []
+        for k in range(PIECES):
+            multiply(LAST_PATH, k)
+            upright_sums.append(flip_back(flipped_sums[k], 0))
+            if k > 0:
+                copy_out(contracted, k - 1, upright_sums[k - 1])
+        copy_out(contracted, PIECES - 1, upright_sums[PIECES - 1])
+
         gated = held.tile([FEATURES, NODES], F32, name="gated")
         for k in range(PIECES):
-            nc.scalar.activation(contracted[:, nodes(k)], sums[k][:], COPY)
-            nc.vector.tensor_tensor(gated[:, nodes(k)], looked_up(PATHS, k), contracted[:, nodes(k)], MULT)
-            nc.sync.dma_start(out[:, nodes(k)], gated[:, nodes(k)])
+            nc.vector.tensor_tensor(gated[:, piece(k)], looked_up(PATHS, k), contracted[:, piece(k)], MULT)
+            nc.sync.dma_start(out[:, piece(k)], gated[:, piece(k)])

@@ -14,7 +14,6 @@ PATHS = 5
 DIMS = 3
 PIECE = 256
 PIECES = NODES // PIECE
-PIECE_OFFSET_COLUMNS = PIECE // 16
 HALF = NODES // 2
 BLOCK = 128
 FIRST_PATH, LAST_PATH = 0, 4
@@ -32,8 +31,8 @@ def tile_equivariantproductbasisblock_kernel(tc, x0, x1, wt, offs, out):
     with (
         tc.tile_pool(name="held", bufs=1) as held,
         tc.tile_pool(name="work", bufs=2) as work,
-        tc.psum_pool(name="sum_banks", bufs=1) as sum_banks,
-        tc.psum_pool(name="turn_banks", bufs=3) as turn_banks,
+        tc.psum_pool(name="flipped_banks", bufs=1) as flipped_banks,
+        tc.psum_pool(name="upright_banks", bufs=2) as upright_banks,
     ):
         offsets = held.tile([FEATURES, NODES // 16], U16, name="offsets")
         nc.sync.dma_start(offsets[:], offs)
@@ -74,15 +73,16 @@ def tile_equivariantproductbasisblock_kernel(tc, x0, x1, wt, offs, out):
                     stop=last and b == blocks - 1,
                 )
 
-        def flip_back(flipped_bank, first_column):
-            flipped = work.tile([BLOCK, PIECE], F32, name="flipped")
-            nc.scalar.activation(flipped[:], flipped_bank[:, first_column : first_column + PIECE], COPY)
-            upright_bank = turn_banks.tile([FEATURES, PIECE], F32, name="upright_bank", tag="turn")
-            flip_onto(upright_bank, flipped, 0, True, True)
-            return upright_bank
-
-        def copy_out(tile, k, upright_bank):
-            nc.scalar.activation(tile[:, piece(k)], upright_bank[:], COPY)
+        def bring_back(tile, first_node, flipped_bank, parts):
+            width = flipped_bank.shape[1] // parts
+            banks = []
+            for i in range(parts):
+                flipped = work.tile([BLOCK, width], F32, name="flipped", tag="flipped")
+                nc.scalar.activation(flipped[:], flipped_bank[:, i * width : (i + 1) * width], COPY)
+                banks.append(upright_banks.tile([FEATURES, width], F32, name="upright", tag="upright"))
+                flip_onto(banks[i], flipped, 0, True, True)
+            for i in range(parts):
+                nc.scalar.activation(tile[:, first_node + i * width : first_node + (i + 1) * width], banks[i][:], COPY)
 
         square = held.tile([FEATURES, NODES], F32, name="square")
         squares = [held.tile([FEATURES, NODES], F32, name=f"squares{d}") for d in range(DIMS)]
@@ -91,50 +91,47 @@ def tile_equivariantproductbasisblock_kernel(tc, x0, x1, wt, offs, out):
         scalar_dot = held.tile([FEATURES, NODES], F32, name="scalar_dot")
         paths = [scalars, square, dot, cube, scalar_dot]
         products = [held.tile([FEATURES, NODES], F32, name=f"products{p}") for p in range(PATHS)]
-        flipped_sums = [sum_banks.tile([BLOCK, PIECE], F32, name=f"flipped_sums{k}") for k in range(PIECES)]
+        flipped_sums = [flipped_banks.tile([BLOCK, PIECE], F32, name=f"flipped_sums{k}") for k in range(PIECES)]
+        flipped_dot = [flipped_banks.tile([BLOCK, HALF], F32, name=f"flipped_dot{h}") for h in range(NODES // HALF)]
 
-        def looked_up(b, k):
-            return tables[b][:].indirect(offsets[:, k * PIECE_OFFSET_COLUMNS : (k + 1) * PIECE_OFFSET_COLUMNS])
+        def looked_up(b, first_node, width):
+            return tables[b][:].indirect(offsets[:, first_node // 16 : (first_node + width) // 16])
 
         def multiply(p, k):
-            nc.vector.tensor_tensor(products[p][:, piece(k)], looked_up(p, k), paths[p][:, piece(k)], MULT)
+            nc.vector.tensor_tensor(products[p][:, piece(k)], looked_up(p, k * PIECE, PIECE), paths[p][:, piece(k)], MULT)
             flip_onto(flipped_sums[k], products[p], k * PIECE, p == FIRST_PATH, p == LAST_PATH)
 
         def contract(p):
             for k in range(PIECES):
                 multiply(p, k)
 
-        def make_dot(h):
-            flipped_dot = turn_banks.tile([BLOCK, HALF], F32, name="flipped_dot", tag="turn")
-            for d in range(DIMS):
-                nc.scalar.activation(squares[d][:, half(h)], vectors[d][:, half(h)], SQUARE)
-                flip_onto(flipped_dot, squares[d], h * HALF, d == 0, d == DIMS - 1)
-            upright_banks = [flip_back(flipped_dot, i * PIECE) for i in range(HALF // PIECE)]
-            for i in range(HALF // PIECE):
-                copy_out(dot, h * (HALF // PIECE) + i, upright_banks[i])
-
         for k in range(PIECES):
             nc.scalar.activation(square[:, piece(k)], scalars[:, piece(k)], SQUARE)
         contract(0)
         nc.vector.tensor_tensor(cube[:], square[:], scalars[:], MULT)
-        make_dot(0)
-        contract(1)
-        make_dot(1)
-        contract(3)
-        contract(2)
-        for h in range(NODES // HALF):
-            nc.vector.tensor_tensor(scalar_dot[:, half(h)], scalars[:, half(h)], dot[:, half(h)], MULT)
 
+        for h in range(NODES // HALF):
+            for d in range(DIMS):
+                nc.scalar.activation(squares[d][:, half(h)], vectors[d][:, half(h)], SQUARE)
+                flip_onto(flipped_dot[h], squares[d], h * HALF, d == 0, d == DIMS - 1)
+        for h in range(NODES // HALF):
+            bring_back(dot, h * HALF, flipped_dot[h], 2)
+
+        contract(1)
+        contract(3)
+
+        parts_of_piece = [1] * (PIECES - 1) + [2]
         contracted = held.tile([FEATURES, NODES], F32, name="contracted")
-        upright_sums = []
         for k in range(PIECES):
+            nc.vector.tensor_tensor(scalar_dot[:, piece(k)], scalars[:, piece(k)], dot[:, piece(k)], MULT)
+            multiply(2, k)
             multiply(LAST_PATH, k)
-            upright_sums.append(flip_back(flipped_sums[k], 0))
-            if k > 0:
-                copy_out(contracted, k - 1, upright_sums[k - 1])
-        copy_out(contracted, PIECES - 1, upright_sums[PIECES - 1])
+            bring_back(contracted, k * PIECE, flipped_sums[k], parts_of_piece[k])
 
         gated = held.tile([FEATURES, NODES], F32, name="gated")
         for k in range(PIECES):
-            nc.vector.tensor_tensor(gated[:, piece(k)], looked_up(PATHS, k), contracted[:, piece(k)], MULT)
-            nc.sync.dma_start(out[:, piece(k)], gated[:, piece(k)])
+            width = PIECE // parts_of_piece[k]
+            for first_node in range(k * PIECE, (k + 1) * PIECE, width):
+                nodes = slice(first_node, first_node + width)
+                nc.vector.tensor_tensor(gated[:, nodes], looked_up(PATHS, first_node, width), contracted[:, nodes], MULT)
+                nc.sync.dma_start(out[:, nodes], gated[:, nodes])

@@ -53,9 +53,8 @@ def tile_equivariantproductbasisblock_kernel(tc, x0, x1, wt, offs, out):
             nc.sync.dma_start(scalars[:, piece(k)], x0[:, piece(k)])
         load_table(nc.sync, 1)
         load_vectors(0)
-        load_table(nc.sync, 3)
         load_vectors(1)
-        for b in (2, 4, PATHS):
+        for b in (3, 2, 4, PATHS):
             load_table(nc.sync, b)
 
         identity = held.tile([FEATURES, FEATURES], F32, name="identity")

@@ -11,10 +11,12 @@ FEATURES = 128
 NODES = 1024
 SPECIES = 256
 PATHS = 5
+GATE = 5
 DIMS = 3
-PIECE = 256
+PIECE = SPECIES
 PIECES = NODES // PIECE
-HALF = NODES // 2
+HALF = 512
+HALVES = NODES // HALF
 BLOCK = 128
 FIRST_PATH, LAST_PATH = 0, 4
 
@@ -30,7 +32,7 @@ def tile_equivariantproductbasisblock_kernel(tc, x0, x1, wt, offs, out):
 
     with (
         tc.tile_pool(name="held", bufs=1) as held,
-        tc.tile_pool(name="work", bufs=2) as work,
+        tc.tile_pool(name="flipped_parts", bufs=2) as flipped_parts,
         tc.psum_pool(name="flipped_banks", bufs=1) as flipped_banks,
         tc.psum_pool(name="upright_banks", bufs=2) as upright_banks,
     ):
@@ -44,17 +46,14 @@ def tile_equivariantproductbasisblock_kernel(tc, x0, x1, wt, offs, out):
         def load_table(queue, b):
             queue.dma_start(tables[b][:], wt[b * FEATURES : (b + 1) * FEATURES, :])
 
-        def load_vectors(h):
-            for d in range(DIMS):
-                nc.sync.dma_start(vectors[d][:, half(h)], x1[d * FEATURES : (d + 1) * FEATURES, half(h)])
-
         load_table(nc.scalar, 0)
         for k in range(PIECES):
             nc.sync.dma_start(scalars[:, piece(k)], x0[:, piece(k)])
         load_table(nc.sync, 1)
-        load_vectors(0)
-        load_vectors(1)
-        for b in (3, 2, 4, PATHS):
+        for h in range(HALVES):
+            for d in range(DIMS):
+                nc.sync.dma_start(vectors[d][:, half(h)], x1[d * FEATURES : (d + 1) * FEATURES, half(h)])
+        for b in (3, 2, 4, GATE):
             load_table(nc.sync, b)
 
         identity = held.tile([FEATURES, FEATURES], F32, name="identity")
@@ -62,36 +61,36 @@ def tile_equivariantproductbasisblock_kernel(tc, x0, x1, wt, offs, out):
 
         def flip_onto(bank, tile, first_column, first, last):
             blocks = bank.shape[1] // BLOCK
-            for b in range(blocks):
+            for i in range(blocks):
                 nc.tensor.matmul(
-                    bank[:, b * BLOCK : (b + 1) * BLOCK],
-                    tile[:, first_column + b * BLOCK : first_column + (b + 1) * BLOCK],
+                    bank[:, i * BLOCK : (i + 1) * BLOCK],
+                    tile[:, first_column + i * BLOCK : first_column + (i + 1) * BLOCK],
                     identity[:],
                     is_transpose=True,
-                    start=first and b == 0,
-                    stop=last and b == blocks - 1,
+                    start=first and i == 0,
+                    stop=last and i == blocks - 1,
                 )
 
         def bring_back(tile, first_node, flipped_bank, parts):
             width = flipped_bank.shape[1] // parts
-            banks = []
+            upright = []
             for i in range(parts):
-                flipped = work.tile([BLOCK, width], F32, name="flipped", tag="flipped")
+                flipped = flipped_parts.tile([BLOCK, width], F32, name="flipped", tag="flipped")
                 nc.scalar.activation(flipped[:], flipped_bank[:, i * width : (i + 1) * width], COPY)
-                banks.append(upright_banks.tile([FEATURES, width], F32, name="upright", tag="upright"))
-                flip_onto(banks[i], flipped, 0, True, True)
+                upright.append(upright_banks.tile([FEATURES, width], F32, name="upright", tag="upright"))
+                flip_onto(upright[i], flipped, 0, True, True)
             for i in range(parts):
-                nc.scalar.activation(tile[:, first_node + i * width : first_node + (i + 1) * width], banks[i][:], COPY)
+                nc.scalar.activation(tile[:, first_node + i * width : first_node + (i + 1) * width], upright[i][:], COPY)
 
-        square = held.tile([FEATURES, NODES], F32, name="square")
-        squares = [held.tile([FEATURES, NODES], F32, name=f"squares{d}") for d in range(DIMS)]
-        cube = held.tile([FEATURES, NODES], F32, name="cube")
+        scalars_squared = held.tile([FEATURES, NODES], F32, name="scalars_squared")
+        scalars_cubed = held.tile([FEATURES, NODES], F32, name="scalars_cubed")
+        vectors_squared = [held.tile([FEATURES, NODES], F32, name=f"vectors_squared{d}") for d in range(DIMS)]
         dot = held.tile([FEATURES, NODES], F32, name="dot")
-        scalar_dot = held.tile([FEATURES, NODES], F32, name="scalar_dot")
-        paths = [scalars, square, dot, cube, scalar_dot]
+        scalars_times_dot = held.tile([FEATURES, NODES], F32, name="scalars_times_dot")
+        paths = [scalars, scalars_squared, dot, scalars_cubed, scalars_times_dot]
         products = [held.tile([FEATURES, NODES], F32, name=f"products{p}") for p in range(PATHS)]
         flipped_sums = [flipped_banks.tile([BLOCK, PIECE], F32, name=f"flipped_sums{k}") for k in range(PIECES)]
-        flipped_dot = [flipped_banks.tile([BLOCK, HALF], F32, name=f"flipped_dot{h}") for h in range(NODES // HALF)]
+        flipped_dot = [flipped_banks.tile([BLOCK, HALF], F32, name=f"flipped_dot{h}") for h in range(HALVES)]
 
         def looked_up(b, first_node, width):
             return tables[b][:].indirect(offsets[:, first_node // 16 : (first_node + width) // 16])
@@ -100,29 +99,27 @@ def tile_equivariantproductbasisblock_kernel(tc, x0, x1, wt, offs, out):
             nc.vector.tensor_tensor(products[p][:, piece(k)], looked_up(p, k * PIECE, PIECE), paths[p][:, piece(k)], MULT)
             flip_onto(flipped_sums[k], products[p], k * PIECE, p == FIRST_PATH, p == LAST_PATH)
 
-        def contract(p):
+        for k in range(PIECES):
+            nc.scalar.activation(scalars_squared[:, piece(k)], scalars[:, piece(k)], SQUARE)
+        for k in range(PIECES):
+            multiply(0, k)
+        nc.vector.tensor_tensor(scalars_cubed[:], scalars_squared[:], scalars[:], MULT)
+
+        for h in range(HALVES):
+            for d in range(DIMS):
+                nc.scalar.activation(vectors_squared[d][:, half(h)], vectors[d][:, half(h)], SQUARE)
+                flip_onto(flipped_dot[h], vectors_squared[d], h * HALF, d == 0, d == DIMS - 1)
+        for h in range(HALVES):
+            bring_back(dot, h * HALF, flipped_dot[h], HALF // PIECE)
+
+        for p in (1, 3):
             for k in range(PIECES):
                 multiply(p, k)
-
-        for k in range(PIECES):
-            nc.scalar.activation(square[:, piece(k)], scalars[:, piece(k)], SQUARE)
-        contract(0)
-        nc.vector.tensor_tensor(cube[:], square[:], scalars[:], MULT)
-
-        for h in range(NODES // HALF):
-            for d in range(DIMS):
-                nc.scalar.activation(squares[d][:, half(h)], vectors[d][:, half(h)], SQUARE)
-                flip_onto(flipped_dot[h], squares[d], h * HALF, d == 0, d == DIMS - 1)
-        for h in range(NODES // HALF):
-            bring_back(dot, h * HALF, flipped_dot[h], 2)
-
-        contract(1)
-        contract(3)
 
         parts_of_piece = [1] * (PIECES - 1) + [2]
         contracted = held.tile([FEATURES, NODES], F32, name="contracted")
         for k in range(PIECES):
-            nc.vector.tensor_tensor(scalar_dot[:, piece(k)], scalars[:, piece(k)], dot[:, piece(k)], MULT)
+            nc.vector.tensor_tensor(scalars_times_dot[:, piece(k)], scalars[:, piece(k)], dot[:, piece(k)], MULT)
             multiply(2, k)
             multiply(LAST_PATH, k)
             bring_back(contracted, k * PIECE, flipped_sums[k], parts_of_piece[k])
@@ -132,5 +129,5 @@ def tile_equivariantproductbasisblock_kernel(tc, x0, x1, wt, offs, out):
             width = PIECE // parts_of_piece[k]
             for first_node in range(k * PIECE, (k + 1) * PIECE, width):
                 nodes = slice(first_node, first_node + width)
-                nc.vector.tensor_tensor(gated[:, nodes], looked_up(PATHS, first_node, width), contracted[:, nodes], MULT)
+                nc.vector.tensor_tensor(gated[:, nodes], looked_up(GATE, first_node, width), contracted[:, nodes], MULT)
                 nc.sync.dma_start(out[:, nodes], gated[:, nodes])

@@ -18,7 +18,7 @@ PIECES = NODES // PIECE
 HALF = 512
 HALVES = NODES // HALF
 BLOCK = 128
-FIRST_PATH, LAST_PATH = 0, 4
+FIRST_FLIPPED, LAST_FLIPPED = 0, 3
 
 
 def tile_equivariantproductbasisblock_kernel(tc, x0, x1, wt, offs, out):
@@ -33,8 +33,7 @@ def tile_equivariantproductbasisblock_kernel(tc, x0, x1, wt, offs, out):
     with (
         tc.tile_pool(name="held", bufs=1) as held,
         tc.tile_pool(name="flipped_parts", bufs=2) as flipped_parts,
-        tc.psum_pool(name="flipped_banks", bufs=1) as flipped_banks,
-        tc.psum_pool(name="upright_banks", bufs=2) as upright_banks,
+        tc.psum_pool(name="banks", bufs=8) as banks,
     ):
         offsets = held.tile([FEATURES, NODES // 16], U16, name="offsets")
         nc.sync.dma_start(offsets[:], offs)
@@ -77,7 +76,7 @@ def tile_equivariantproductbasisblock_kernel(tc, x0, x1, wt, offs, out):
             for i in range(parts):
                 flipped = flipped_parts.tile([BLOCK, width], F32, name="flipped", tag="flipped")
                 nc.scalar.activation(flipped[:], flipped_bank[:, i * width : (i + 1) * width], COPY)
-                upright.append(upright_banks.tile([FEATURES, width], F32, name="upright", tag="upright"))
+                upright.append(banks.tile([FEATURES, width], F32, name="upright", tag="bank"))
                 flip_onto(upright[i], flipped, 0, True, True)
             for i in range(parts):
                 nc.scalar.activation(tile[:, first_node + i * width : first_node + (i + 1) * width], upright[i][:], COPY)
@@ -89,20 +88,43 @@ def tile_equivariantproductbasisblock_kernel(tc, x0, x1, wt, offs, out):
         scalars_times_dot = held.tile([FEATURES, NODES], F32, name="scalars_times_dot")
         paths = [scalars, scalars_squared, dot, scalars_cubed, scalars_times_dot]
         products = [held.tile([FEATURES, NODES], F32, name=f"products{p}") for p in range(PATHS)]
-        flipped_sums = [flipped_banks.tile([BLOCK, PIECE], F32, name=f"flipped_sums{k}") for k in range(PIECES)]
-        flipped_dot = [flipped_banks.tile([BLOCK, HALF], F32, name=f"flipped_dot{h}") for h in range(HALVES)]
+        flipped_sums = [banks.tile([BLOCK, PIECE], F32, name=f"flipped_sums{k}", tag="bank") for k in range(PIECES)]
+        flipped_dot = [banks.tile([BLOCK, HALF], F32, name=f"flipped_dot{h}", tag="bank") for h in range(HALVES)]
 
         def looked_up(b, first_node, width):
             return tables[b][:].indirect(offsets[:, first_node // 16 : (first_node + width) // 16])
 
         def multiply(p, k):
             nc.vector.tensor_tensor(products[p][:, piece(k)], looked_up(p, k * PIECE, PIECE), paths[p][:, piece(k)], MULT)
-            flip_onto(flipped_sums[k], products[p], k * PIECE, p == FIRST_PATH, p == LAST_PATH)
+
+        def multiply_and_add_flipped(p, k):
+            multiply(p, k)
+            flip_onto(flipped_sums[k], products[p], k * PIECE, p == FIRST_FLIPPED, p == LAST_FLIPPED)
+
+        parts_of_piece = [1] * (PIECES - 1) + [2]
+        contracted_banks = [[] for k in range(PIECES)]
+
+        def open_contracted(k):
+            flipped = flipped_parts.tile([BLOCK, PIECE], F32, name="flipped", tag="flipped")
+            nc.scalar.activation(flipped[:], flipped_sums[k][:], COPY)
+            width = PIECE // parts_of_piece[k]
+            for i in range(parts_of_piece[k]):
+                contracted_banks[k].append(banks.tile([FEATURES, width], F32, name="contracted_bank", tag="bank"))
+                flip_onto(contracted_banks[k][i], flipped, i * width, True, False)
+
+        def multiply_and_add_upright(p, k, last):
+            multiply(p, k)
+            width = PIECE // parts_of_piece[k]
+            for i in range(parts_of_piece[k]):
+                first_node = k * PIECE + i * width
+                nc.tensor.matmul(
+                    contracted_banks[k][i][:], identity[:], products[p][:, first_node : first_node + width], start=False, stop=last
+                )
 
         for k in range(PIECES):
             nc.scalar.activation(scalars_squared[:, piece(k)], scalars[:, piece(k)], SQUARE)
         for k in range(PIECES):
-            multiply(0, k)
+            multiply_and_add_flipped(0, k)
         nc.vector.tensor_tensor(scalars_cubed[:], scalars_squared[:], scalars[:], MULT)
 
         for h in range(HALVES):
@@ -112,17 +134,21 @@ def tile_equivariantproductbasisblock_kernel(tc, x0, x1, wt, offs, out):
         for h in range(HALVES):
             bring_back(dot, h * HALF, flipped_dot[h], HALF // PIECE)
 
-        for p in (1, 3):
-            for k in range(PIECES):
-                multiply(p, k)
+        for k in range(PIECES):
+            multiply_and_add_flipped(1, k)
+        for k in range(PIECES):
+            multiply_and_add_flipped(LAST_FLIPPED, k)
+            open_contracted(k)
 
-        parts_of_piece = [1] * (PIECES - 1) + [2]
         contracted = held.tile([FEATURES, NODES], F32, name="contracted")
         for k in range(PIECES):
             nc.vector.tensor_tensor(scalars_times_dot[:, piece(k)], scalars[:, piece(k)], dot[:, piece(k)], MULT)
-            multiply(2, k)
-            multiply(LAST_PATH, k)
-            bring_back(contracted, k * PIECE, flipped_sums[k], parts_of_piece[k])
+            multiply_and_add_upright(2, k, False)
+            multiply_and_add_upright(4, k, True)
+            width = PIECE // parts_of_piece[k]
+            for i in range(parts_of_piece[k]):
+                first_node = k * PIECE + i * width
+                nc.scalar.activation(contracted[:, first_node : first_node + width], contracted_banks[k][i][:], COPY)
 
         gated = held.tile([FEATURES, NODES], F32, name="gated")
         for k in range(PIECES):

@@ -70,17 +70,6 @@ def tile_equivariantproductbasisblock_kernel(tc, x0, x1, wt, offs, out):
                     stop=last and i == blocks - 1,
                 )
 
-        def bring_back(tile, first_node, flipped_bank, parts):
-            width = flipped_bank.shape[1] // parts
-            upright = []
-            for i in range(parts):
-                flipped = flipped_parts.tile([BLOCK, width], F32, name="flipped", tag="flipped")
-                nc.scalar.activation(flipped[:], flipped_bank[:, i * width : (i + 1) * width], COPY)
-                upright.append(banks.tile([FEATURES, width], F32, name="upright", tag="bank"))
-                flip_onto(upright[i], flipped, 0, True, True)
-            for i in range(parts):
-                nc.scalar.activation(tile[:, first_node + i * width : first_node + (i + 1) * width], upright[i][:], COPY)
-
         scalars_squared = held.tile([FEATURES, NODES], F32, name="scalars_squared")
         scalars_cubed = held.tile([FEATURES, NODES], F32, name="scalars_cubed")
         vectors_squared = [held.tile([FEATURES, NODES], F32, name=f"vectors_squared{d}") for d in range(DIMS)]
@@ -89,13 +78,16 @@ def tile_equivariantproductbasisblock_kernel(tc, x0, x1, wt, offs, out):
         paths = [scalars, scalars_squared, dot, scalars_cubed, scalars_times_dot]
         products = [held.tile([FEATURES, NODES], F32, name=f"products{p}") for p in range(PATHS)]
         flipped_sums = [banks.tile([BLOCK, PIECE], F32, name=f"flipped_sums{k}", tag="bank") for k in range(PIECES)]
-        flipped_dot = [banks.tile([BLOCK, HALF], F32, name=f"flipped_dot{h}", tag="bank") for h in range(HALVES)]
 
         def looked_up(b, first_node, width):
             return tables[b][:].indirect(offsets[:, first_node // 16 : (first_node + width) // 16])
 
+        def multiply_nodes(p, first_node, width):
+            nodes = slice(first_node, first_node + width)
+            nc.vector.tensor_tensor(products[p][:, nodes], looked_up(p, first_node, width), paths[p][:, nodes], MULT)
+
         def multiply(p, k):
-            nc.vector.tensor_tensor(products[p][:, piece(k)], looked_up(p, k * PIECE, PIECE), paths[p][:, piece(k)], MULT)
+            multiply_nodes(p, k * PIECE, PIECE)
 
         def multiply_and_add_flipped(p, k):
             multiply(p, k)
@@ -113,10 +105,13 @@ def tile_equivariantproductbasisblock_kernel(tc, x0, x1, wt, offs, out):
                 flip_onto(contracted_banks[k][i], flipped, i * width, True, False)
 
         def multiply_and_add_upright(p, k, last):
-            multiply(p, k)
             width = PIECE // parts_of_piece[k]
+            if not last:
+                multiply(p, k)
             for i in range(parts_of_piece[k]):
                 first_node = k * PIECE + i * width
+                if last:
+                    multiply_nodes(p, first_node, width)
                 nc.tensor.matmul(
                     contracted_banks[k][i][:], identity[:], products[p][:, first_node : first_node + width], start=False, stop=last
                 )
@@ -127,12 +122,24 @@ def tile_equivariantproductbasisblock_kernel(tc, x0, x1, wt, offs, out):
             multiply_and_add_flipped(0, k)
         nc.vector.tensor_tensor(scalars_cubed[:], scalars_squared[:], scalars[:], MULT)
 
-        for h in range(HALVES):
-            for d in range(DIMS):
-                nc.scalar.activation(vectors_squared[d][:, half(h)], vectors[d][:, half(h)], SQUARE)
-                flip_onto(flipped_dot[h], vectors_squared[d], h * HALF, d == 0, d == DIMS - 1)
-        for h in range(HALVES):
-            bring_back(dot, h * HALF, flipped_dot[h], HALF // PIECE)
+        flipped_dot = [None] * PIECES
+        upright_dot = [None] * PIECES
+        for step in range(PIECES + 2):
+            if step < PIECES:
+                k = step
+                flipped_dot[k] = banks.tile([BLOCK, PIECE], F32, name="flipped_dot", tag="bank")
+                for d in range(DIMS):
+                    nc.scalar.activation(vectors_squared[d][:, piece(k)], vectors[d][:, piece(k)], SQUARE)
+                    flip_onto(flipped_dot[k], vectors_squared[d], k * PIECE, d == 0, d == DIMS - 1)
+            if 1 <= step <= PIECES:
+                k = step - 1
+                flipped = flipped_parts.tile([BLOCK, PIECE], F32, name="flipped", tag="flipped")
+                nc.scalar.activation(flipped[:], flipped_dot[k][:], COPY)
+                upright_dot[k] = banks.tile([FEATURES, PIECE], F32, name="upright_dot", tag="bank")
+                flip_onto(upright_dot[k], flipped, 0, True, True)
+            if step >= 2:
+                k = step - 2
+                nc.scalar.activation(dot[:, piece(k)], upright_dot[k][:], COPY)
 
         for k in range(PIECES):
             multiply_and_add_flipped(1, k)

@@ -82,12 +82,8 @@ def tile_equivariantproductbasisblock_kernel(tc, x0, x1, wt, offs, out):
         def looked_up(b, first_node, width):
             return tables[b][:].indirect(offsets[:, first_node // 16 : (first_node + width) // 16])
 
-        def multiply_nodes(p, first_node, width):
-            nodes = slice(first_node, first_node + width)
-            nc.vector.tensor_tensor(products[p][:, nodes], looked_up(p, first_node, width), paths[p][:, nodes], MULT)
-
         def multiply(p, k):
-            multiply_nodes(p, k * PIECE, PIECE)
+            nc.vector.tensor_tensor(products[p][:, piece(k)], looked_up(p, k * PIECE, PIECE), paths[p][:, piece(k)], MULT)
 
         def multiply_and_add_flipped(p, k):
             multiply(p, k)
@@ -105,13 +101,10 @@ def tile_equivariantproductbasisblock_kernel(tc, x0, x1, wt, offs, out):
                 flip_onto(contracted_banks[k][i], flipped, i * width, True, False)
 
         def multiply_and_add_upright(p, k, last):
+            multiply(p, k)
             width = PIECE // parts_of_piece[k]
-            if not last:
-                multiply(p, k)
             for i in range(parts_of_piece[k]):
                 first_node = k * PIECE + i * width
-                if last:
-                    multiply_nodes(p, first_node, width)
                 nc.tensor.matmul(
                     contracted_banks[k][i][:], identity[:], products[p][:, first_node : first_node + width], start=False, stop=last
                 )
@@ -143,19 +136,23 @@ def tile_equivariantproductbasisblock_kernel(tc, x0, x1, wt, offs, out):
 
         for k in range(PIECES):
             multiply_and_add_flipped(1, k)
-        for k in range(PIECES):
-            multiply_and_add_flipped(LAST_FLIPPED, k)
-            open_contracted(k)
 
+        BEHIND = 2
         contracted = held.tile([FEATURES, NODES], F32, name="contracted")
-        for k in range(PIECES):
-            nc.vector.tensor_tensor(scalars_times_dot[:, piece(k)], scalars[:, piece(k)], dot[:, piece(k)], MULT)
-            multiply_and_add_upright(2, k, False)
-            multiply_and_add_upright(4, k, True)
-            width = PIECE // parts_of_piece[k]
-            for i in range(parts_of_piece[k]):
-                first_node = k * PIECE + i * width
-                nc.scalar.activation(contracted[:, first_node : first_node + width], contracted_banks[k][i][:], COPY)
+        for step in range(PIECES + BEHIND):
+            if step < PIECES:
+                k = step
+                multiply_and_add_flipped(LAST_FLIPPED, k)
+                open_contracted(k)
+            if step >= BEHIND:
+                k = step - BEHIND
+                nc.vector.tensor_tensor(scalars_times_dot[:, piece(k)], scalars[:, piece(k)], dot[:, piece(k)], MULT)
+                multiply_and_add_upright(2, k, False)
+                multiply_and_add_upright(4, k, True)
+                width = PIECE // parts_of_piece[k]
+                for i in range(parts_of_piece[k]):
+                    first_node = k * PIECE + i * width
+                    nc.scalar.activation(contracted[:, first_node : first_node + width], contracted_banks[k][i][:], COPY)
 
         gated = held.tile([FEATURES, NODES], F32, name="gated")
         for k in range(PIECES):

@@ -70,6 +70,17 @@ def tile_equivariantproductbasisblock_kernel(tc, x0, x1, wt, offs, out):
                     stop=last and i == blocks - 1,
                 )
 
+        def flip_by_matmul_onto(bank, tile):
+            blocks = bank.shape[1] // BLOCK
+            for i in range(blocks):
+                nc.tensor.matmul(
+                    bank[:, i * BLOCK : (i + 1) * BLOCK],
+                    tile[:, i * BLOCK : (i + 1) * BLOCK],
+                    identity[:],
+                    start=i == 0,
+                    stop=i == blocks - 1,
+                )
+
         scalars_squared = held.tile([FEATURES, NODES], F32, name="scalars_squared")
         scalars_cubed = held.tile([FEATURES, NODES], F32, name="scalars_cubed")
         vectors_squared = [held.tile([FEATURES, NODES], F32, name=f"vectors_squared{d}") for d in range(DIMS)]
@@ -129,7 +140,7 @@ def tile_equivariantproductbasisblock_kernel(tc, x0, x1, wt, offs, out):
                 flipped = flipped_parts.tile([BLOCK, PIECE], F32, name="flipped", tag="flipped")
                 nc.scalar.activation(flipped[:], flipped_dot[k][:], COPY)
                 upright_dot[k] = banks.tile([FEATURES, PIECE], F32, name="upright_dot", tag="bank")
-                flip_onto(upright_dot[k], flipped, 0, True, True)
+                flip_by_matmul_onto(upright_dot[k], flipped)
             if step >= 2:
                 k = step - 2
                 nc.scalar.activation(dot[:, piece(k)], upright_dot[k][:], COPY)

@@ -70,15 +70,15 @@ def tile_equivariantproductbasisblock_kernel(tc, x0, x1, wt, offs, out):
                     stop=last and i == blocks - 1,
                 )
 
-        def flip_by_matmul_onto(bank, tile):
+        def flip_by_matmul_onto(bank, tile, first_column, last):
             blocks = bank.shape[1] // BLOCK
             for i in range(blocks):
                 nc.tensor.matmul(
                     bank[:, i * BLOCK : (i + 1) * BLOCK],
-                    tile[:, i * BLOCK : (i + 1) * BLOCK],
+                    tile[:, first_column + i * BLOCK : first_column + (i + 1) * BLOCK],
                     identity[:],
                     start=i == 0,
-                    stop=i == blocks - 1,
+                    stop=last and i == blocks - 1,
                 )
 
         scalars_squared = held.tile([FEATURES, NODES], F32, name="scalars_squared")
@@ -123,7 +123,11 @@ def tile_equivariantproductbasisblock_kernel(tc, x0, x1, wt, offs, out):
         for k in range(PIECES):
             nc.scalar.activation(scalars_squared[:, piece(k)], scalars[:, piece(k)], SQUARE)
         for k in range(PIECES):
-            multiply_and_add_flipped(0, k)
+            if k < PIECES // 2:
+                multiply(FIRST_FLIPPED, k)
+                flip_by_matmul_onto(flipped_sums[k], products[FIRST_FLIPPED], k * PIECE, False)
+            else:
+                multiply_and_add_flipped(FIRST_FLIPPED, k)
         nc.vector.tensor_tensor(scalars_cubed[:], scalars_squared[:], scalars[:], MULT)
 
         flipped_dot = [None] * PIECES
@@ -140,7 +144,7 @@ def tile_equivariantproductbasisblock_kernel(tc, x0, x1, wt, offs, out):
                 flipped = flipped_parts.tile([BLOCK, PIECE], F32, name="flipped", tag="flipped")
                 nc.scalar.activation(flipped[:], flipped_dot[k][:], COPY)
                 upright_dot[k] = banks.tile([FEATURES, PIECE], F32, name="upright_dot", tag="bank")
-                flip_by_matmul_onto(upright_dot[k], flipped)
+                flip_by_matmul_onto(upright_dot[k], flipped, 0, True)
             if step >= 2:
                 k = step - 2
                 nc.scalar.activation(dot[:, piece(k)], upright_dot[k][:], COPY)
@@ -148,22 +152,19 @@ def tile_equivariantproductbasisblock_kernel(tc, x0, x1, wt, offs, out):
         for k in range(PIECES):
             multiply_and_add_flipped(1, k)
 
-        BEHIND = 2
+        for k in range(PIECES):
+            multiply_and_add_flipped(LAST_FLIPPED, k)
+            open_contracted(k)
+
         contracted = held.tile([FEATURES, NODES], F32, name="contracted")
-        for step in range(PIECES + BEHIND):
-            if step < PIECES:
-                k = step
-                multiply_and_add_flipped(LAST_FLIPPED, k)
-                open_contracted(k)
-            if step >= BEHIND:
-                k = step - BEHIND
-                nc.vector.tensor_tensor(scalars_times_dot[:, piece(k)], scalars[:, piece(k)], dot[:, piece(k)], MULT)
-                multiply_and_add_upright(2, k, False)
-                multiply_and_add_upright(4, k, True)
-                width = PIECE // parts_of_piece[k]
-                for i in range(parts_of_piece[k]):
-                    first_node = k * PIECE + i * width
-                    nc.scalar.activation(contracted[:, first_node : first_node + width], contracted_banks[k][i][:], COPY)
+        for k in range(PIECES):
+            nc.vector.tensor_tensor(scalars_times_dot[:, piece(k)], scalars[:, piece(k)], dot[:, piece(k)], MULT)
+            multiply_and_add_upright(2, k, False)
+            multiply_and_add_upright(4, k, True)
+            width = PIECE // parts_of_piece[k]
+            for i in range(parts_of_piece[k]):
+                first_node = k * PIECE + i * width
+                nc.scalar.activation(contracted[:, first_node : first_node + width], contracted_banks[k][i][:], COPY)
 
         gated = held.tile([FEATURES, NODES], F32, name="gated")
         for k in range(PIECES):

@@ -123,11 +123,8 @@ def tile_equivariantproductbasisblock_kernel(tc, x0, x1, wt, offs, out):
         for k in range(PIECES):
             nc.scalar.activation(scalars_squared[:, piece(k)], scalars[:, piece(k)], SQUARE)
         for k in range(PIECES):
-            if k < PIECES // 2:
-                multiply(FIRST_FLIPPED, k)
-                flip_by_matmul_onto(flipped_sums[k], products[FIRST_FLIPPED], k * PIECE, False)
-            else:
-                multiply_and_add_flipped(FIRST_FLIPPED, k)
+            multiply(FIRST_FLIPPED, k)
+            flip_by_matmul_onto(flipped_sums[k], products[FIRST_FLIPPED], k * PIECE, False)
         nc.vector.tensor_tensor(scalars_cubed[:], scalars_squared[:], scalars[:], MULT)
 
         flipped_dot = [None] * PIECES

@@ -18,7 +18,7 @@ PIECES = NODES // PIECE
 HALF = 512
 HALVES = NODES // HALF
 BLOCK = 128
-FIRST_FLIPPED, LAST_FLIPPED = 0, 3
+BLOCKS = PIECE // BLOCK
 
 
 def tile_equivariantproductbasisblock_kernel(tc, x0, x1, wt, offs, out):
@@ -33,6 +33,7 @@ def tile_equivariantproductbasisblock_kernel(tc, x0, x1, wt, offs, out):
     with (
         tc.tile_pool(name="held", bufs=1) as held,
         tc.tile_pool(name="flipped_parts", bufs=2) as flipped_parts,
+        tc.tile_pool(name="squared_parts", bufs=2) as squared_parts,
         tc.psum_pool(name="banks", bufs=8) as banks,
     ):
         offsets = held.tile([FEATURES, NODES // 16], U16, name="offsets")
@@ -40,132 +41,123 @@ def tile_equivariantproductbasisblock_kernel(tc, x0, x1, wt, offs, out):
 
         tables = [held.tile([FEATURES, SPECIES], F32, name=f"table{b}") for b in range(PATHS + 1)]
         scalars = held.tile([FEATURES, NODES], F32, name="scalars")
-        vectors = [held.tile([FEATURES, NODES], F32, name=f"vectors{d}") for d in range(DIMS)]
+        vectors = held.tile([FEATURES, DIMS, NODES], F32, name="vectors")
+        components = x1.rearrange("(d f) n -> f d n", d=DIMS)
 
         def load_table(queue, b):
             queue.dma_start(tables[b][:], wt[b * FEATURES : (b + 1) * FEATURES, :])
 
-        load_table(nc.scalar, 0)
+        load_table(nc.scalar, 1)
         for k in range(PIECES):
             nc.sync.dma_start(scalars[:, piece(k)], x0[:, piece(k)])
-        load_table(nc.sync, 1)
-        for h in range(HALVES):
-            for d in range(DIMS):
-                nc.sync.dma_start(vectors[d][:, half(h)], x1[d * FEATURES : (d + 1) * FEATURES, half(h)])
-        for b in (3, 2, 4, GATE):
+        for k in range(PIECES):
+            nc.sync.dma_start(vectors[:, :, piece(k)], components[:, :, piece(k)])
+            if k == 0:
+                load_table(nc.sync, 3)
+        for b in (0, 4, 2, GATE):
             load_table(nc.sync, b)
 
         identity = held.tile([FEATURES, FEATURES], F32, name="identity")
         make_identity(nc, identity[:])
 
-        def flip_onto(bank, tile, first_column, first, last):
-            blocks = bank.shape[1] // BLOCK
-            for i in range(blocks):
-                nc.tensor.matmul(
-                    bank[:, i * BLOCK : (i + 1) * BLOCK],
-                    tile[:, first_column + i * BLOCK : first_column + (i + 1) * BLOCK],
-                    identity[:],
-                    is_transpose=True,
-                    start=first and i == 0,
-                    stop=last and i == blocks - 1,
-                )
-
-        def flip_by_matmul_onto(bank, tile, first_column, last):
-            blocks = bank.shape[1] // BLOCK
-            for i in range(blocks):
-                nc.tensor.matmul(
-                    bank[:, i * BLOCK : (i + 1) * BLOCK],
-                    tile[:, first_column + i * BLOCK : first_column + (i + 1) * BLOCK],
-                    identity[:],
-                    start=i == 0,
-                    stop=last and i == blocks - 1,
-                )
+        def flip_block(target, block, plain, start, stop):
+            nc.tensor.matmul(target, block, identity[:], is_transpose=not plain, start=start, stop=stop)
 
         scalars_squared = held.tile([FEATURES, NODES], F32, name="scalars_squared")
-        scalars_cubed = held.tile([FEATURES, NODES], F32, name="scalars_cubed")
-        vectors_squared = [held.tile([FEATURES, NODES], F32, name=f"vectors_squared{d}") for d in range(DIMS)]
         dot = held.tile([FEATURES, NODES], F32, name="dot")
-        scalars_times_dot = held.tile([FEATURES, NODES], F32, name="scalars_times_dot")
-        paths = [scalars, scalars_squared, dot, scalars_cubed, scalars_times_dot]
+        factors = [scalars, scalars, dot, scalars_squared, dot]
         products = [held.tile([FEATURES, NODES], F32, name=f"products{p}") for p in range(PATHS)]
-        flipped_sums = [banks.tile([BLOCK, PIECE], F32, name=f"flipped_sums{k}", tag="bank") for k in range(PIECES)]
 
         def looked_up(b, first_node, width):
             return tables[b][:].indirect(offsets[:, first_node // 16 : (first_node + width) // 16])
 
         def multiply(p, k):
-            nc.vector.tensor_tensor(products[p][:, piece(k)], looked_up(p, k * PIECE, PIECE), paths[p][:, piece(k)], MULT)
+            nc.vector.tensor_tensor(products[p][:, piece(k)], looked_up(p, k * PIECE, PIECE), factors[p][:, piece(k)], MULT)
 
-        def multiply_and_add_flipped(p, k):
-            multiply(p, k)
-            flip_onto(flipped_sums[k], products[p], k * PIECE, p == FIRST_FLIPPED, p == LAST_FLIPPED)
-
-        parts_of_piece = [1] * (PIECES - 1) + [2]
-        contracted_banks = [[] for k in range(PIECES)]
-
-        def open_contracted(k):
-            flipped = flipped_parts.tile([BLOCK, PIECE], F32, name="flipped", tag="flipped")
-            nc.scalar.activation(flipped[:], flipped_sums[k][:], COPY)
-            width = PIECE // parts_of_piece[k]
-            for i in range(parts_of_piece[k]):
-                contracted_banks[k].append(banks.tile([FEATURES, width], F32, name="contracted_bank", tag="bank"))
-                flip_onto(contracted_banks[k][i], flipped, i * width, True, False)
-
-        def multiply_and_add_upright(p, k, last):
-            multiply(p, k)
-            width = PIECE // parts_of_piece[k]
-            for i in range(parts_of_piece[k]):
-                first_node = k * PIECE + i * width
-                nc.tensor.matmul(
-                    contracted_banks[k][i][:], identity[:], products[p][:, first_node : first_node + width], start=False, stop=last
+        def flip_piece_onto(bank, tile, first_node, one_plain, first, last):
+            for i in range(BLOCKS):
+                node = first_node + i * BLOCK
+                flip_block(
+                    bank[:, i * BLOCK : (i + 1) * BLOCK],
+                    tile[:, node : node + BLOCK],
+                    plain=one_plain and i == 0,
+                    start=first and i == 0,
+                    stop=last and i == BLOCKS - 1,
                 )
 
-        for k in range(PIECES):
-            nc.scalar.activation(scalars_squared[:, piece(k)], scalars[:, piece(k)], SQUARE)
-        for k in range(PIECES):
-            multiply(FIRST_FLIPPED, k)
-            flip_by_matmul_onto(flipped_sums[k], products[FIRST_FLIPPED], k * PIECE, False)
-        nc.vector.tensor_tensor(scalars_cubed[:], scalars_squared[:], scalars[:], MULT)
+        brackets = [banks.tile([BLOCK, PIECE], F32, name=f"bracket{k}", tag="bank") for k in range(PIECES)]
 
         flipped_dot = [None] * PIECES
         upright_dot = [None] * PIECES
-        for step in range(PIECES + 2):
+
+        def step_of_dot(step):
             if step < PIECES:
                 k = step
                 flipped_dot[k] = banks.tile([BLOCK, PIECE], F32, name="flipped_dot", tag="bank")
+                squares = squared_parts.tile([FEATURES, DIMS, PIECE], F32, name="squares")
                 for d in range(DIMS):
-                    nc.scalar.activation(vectors_squared[d][:, piece(k)], vectors[d][:, piece(k)], SQUARE)
-                    flip_onto(flipped_dot[k], vectors_squared[d], k * PIECE, d == 0, d == DIMS - 1)
+                    nc.scalar.activation(squares[:, d, :], vectors[:, d, piece(k)], SQUARE)
+                    flip_piece_onto(flipped_dot[k], squares[:, d, :], 0, False, d == 0, d == DIMS - 1)
             if 1 <= step <= PIECES:
                 k = step - 1
                 flipped = flipped_parts.tile([BLOCK, PIECE], F32, name="flipped", tag="flipped")
                 nc.scalar.activation(flipped[:], flipped_dot[k][:], COPY)
                 upright_dot[k] = banks.tile([FEATURES, PIECE], F32, name="upright_dot", tag="bank")
-                flip_by_matmul_onto(upright_dot[k], flipped, 0, True)
+                flip_piece_onto(upright_dot[k], flipped, 0, True, True, True)
             if step >= 2:
                 k = step - 2
                 nc.scalar.activation(dot[:, piece(k)], upright_dot[k][:], COPY)
 
-        for k in range(PIECES):
-            multiply_and_add_flipped(1, k)
+        scalars_flipped = held.tile([BLOCK, NODES], F32, name="scalars_flipped")
+        for h in range(HALVES):
+            flipped_bank = banks.tile([BLOCK, HALF], F32, name="flipped_bank", tag="bank")
+            for column in range(0, HALF, BLOCK):
+                node = h * HALF + column
+                flip_block(
+                    flipped_bank[:, column : column + BLOCK],
+                    scalars[:, node : node + BLOCK],
+                    plain=False,
+                    start=column == 0,
+                    stop=column == HALF - BLOCK,
+                )
+            nc.scalar.activation(scalars_flipped[:, half(h)], flipped_bank[:], COPY)
 
         for k in range(PIECES):
-            multiply_and_add_flipped(LAST_FLIPPED, k)
-            open_contracted(k)
+            nc.scalar.activation(scalars_squared[:, piece(k)], scalars[:, piece(k)], SQUARE)
 
+        lookups = [(p, k) for p in (1, 3, 0) for k in range(PIECES)]
+        for step in range(PIECES + 2):
+            for p, k in lookups[2 * step : 2 * step + 2]:
+                multiply(p, k)
+                if p != 0:
+                    flip_piece_onto(brackets[k], products[p], k * PIECE, p == 1, p == 1, False)
+            step_of_dot(step)
+
+        bracket_products = held.tile([BLOCK, NODES], F32, name="bracket_products")
         contracted = held.tile([FEATURES, NODES], F32, name="contracted")
-        for k in range(PIECES):
-            nc.vector.tensor_tensor(scalars_times_dot[:, piece(k)], scalars[:, piece(k)], dot[:, piece(k)], MULT)
-            multiply_and_add_upright(2, k, False)
-            multiply_and_add_upright(4, k, True)
-            width = PIECE // parts_of_piece[k]
-            for i in range(parts_of_piece[k]):
-                first_node = k * PIECE + i * width
-                nc.scalar.activation(contracted[:, first_node : first_node + width], contracted_banks[k][i][:], COPY)
+        rests_copied = [None] * PIECES
+        for step in range(PIECES + 1):
+            if step < PIECES:
+                k = step
+                multiply(4, k)
+                flip_piece_onto(brackets[k], products[4], k * PIECE, False, False, True)
+                multiply(2, k)
+                rest = banks.tile([BLOCK, PIECE], F32, name="rest", tag="bank")
+                flip_piece_onto(rest, products[0], k * PIECE, False, True, False)
+                flip_piece_onto(rest, products[2], k * PIECE, False, False, True)
+                rests_copied[k] = flipped_parts.tile([BLOCK, PIECE], F32, name="rest_copied", tag="flipped")
+                nc.scalar.activation(rests_copied[k][:], rest[:], COPY)
+            if step >= 1:
+                k = step - 1
+                nc.vector.tensor_tensor(bracket_products[:, piece(k)], brackets[k][:], scalars_flipped[:, piece(k)], MULT)
+                contracted_bank = banks.tile([FEATURES, PIECE], F32, name="contracted_bank", tag="bank")
+                flip_piece_onto(contracted_bank, rests_copied[k], 0, False, True, False)
+                flip_piece_onto(contracted_bank, bracket_products, k * PIECE, False, False, True)
+                nc.scalar.activation(contracted[:, piece(k)], contracted_bank[:], COPY)
 
         gated = held.tile([FEATURES, NODES], F32, name="gated")
         for k in range(PIECES):
-            width = PIECE // parts_of_piece[k]
+            width = PIECE if k < PIECES - 1 else BLOCK
             for first_node in range(k * PIECE, (k + 1) * PIECE, width):
                 nodes = slice(first_node, first_node + width)
                 nc.vector.tensor_tensor(gated[:, nodes], looked_up(GATE, first_node, width), contracted[:, nodes], MULT)

@@ -15,8 +15,6 @@ GATE = 5
 DIMS = 3
 PIECE = SPECIES
 PIECES = NODES // PIECE
-HALF = 512
-HALVES = NODES // HALF
 BLOCK = 128
 BLOCKS = PIECE // BLOCK
 
@@ -27,9 +25,6 @@ def tile_equivariantproductbasisblock_kernel(tc, x0, x1, wt, offs, out):
     def piece(k):
         return slice(k * PIECE, (k + 1) * PIECE)
 
-    def half(h):
-        return slice(h * HALF, (h + 1) * HALF)
-
     with (
         tc.tile_pool(name="held", bufs=1) as held,
         tc.tile_pool(name="flipped_parts", bufs=2) as flipped_parts,
@@ -39,9 +34,12 @@ def tile_equivariantproductbasisblock_kernel(tc, x0, x1, wt, offs, out):
         offsets = held.tile([FEATURES, NODES // 16], U16, name="offsets")
         nc.sync.dma_start(offsets[:], offs)
 
+        def held_tile(name, tag=None):
+            return held.tile([FEATURES, PIECE], F32, name=name, tag=tag or name)
+
         tables = [held.tile([FEATURES, SPECIES], F32, name=f"table{b}") for b in range(PATHS + 1)]
-        scalars = held.tile([FEATURES, NODES], F32, name="scalars")
-        vectors = held.tile([FEATURES, DIMS, NODES], F32, name="vectors")
+        scalars = [held_tile(f"scalars{k}") for k in range(PIECES)]
+        vectors = [held.tile([FEATURES, DIMS, PIECE], F32, name=f"vectors{k}") for k in range(PIECES)]
         components = x1.rearrange("(d f) n -> f d n", d=DIMS)
 
         def load_table(queue, b):
@@ -49,9 +47,9 @@ def tile_equivariantproductbasisblock_kernel(tc, x0, x1, wt, offs, out):
 
         load_table(nc.scalar, 1)
         for k in range(PIECES):
-            nc.sync.dma_start(scalars[:, piece(k)], x0[:, piece(k)])
+            nc.sync.dma_start(scalars[k][:], x0[:, piece(k)])
         for k in range(PIECES):
-            nc.sync.dma_start(vectors[:, :, piece(k)], components[:, :, piece(k)])
+            nc.sync.dma_start(vectors[k][:], components[:, :, piece(k)])
             if k == 0:
                 load_table(nc.sync, 3)
         for b in (0, 4, 2, GATE):
@@ -60,105 +58,97 @@ def tile_equivariantproductbasisblock_kernel(tc, x0, x1, wt, offs, out):
         identity = held.tile([FEATURES, FEATURES], F32, name="identity")
         make_identity(nc, identity[:])
 
-        def flip_block(target, block, plain, start, stop):
-            nc.tensor.matmul(target, block, identity[:], is_transpose=not plain, start=start, stop=stop)
-
-        scalars_squared = held.tile([FEATURES, NODES], F32, name="scalars_squared")
-        dot = held.tile([FEATURES, NODES], F32, name="dot")
-        factors = [scalars, scalars, dot, scalars_squared, dot]
-        products = [held.tile([FEATURES, NODES], F32, name=f"products{p}") for p in range(PATHS)]
-
-        def looked_up(b, first_node, width):
-            return tables[b][:].indirect(offsets[:, first_node // 16 : (first_node + width) // 16])
-
-        def multiply(p, k):
-            nc.vector.tensor_tensor(products[p][:, piece(k)], looked_up(p, k * PIECE, PIECE), factors[p][:, piece(k)], MULT)
-
-        def flip_piece_onto(bank, tile, first_node, one_plain, first, last):
+        def flip_onto(bank, tile, first, last, one_plain=False):
             for i in range(BLOCKS):
-                node = first_node + i * BLOCK
-                flip_block(
-                    bank[:, i * BLOCK : (i + 1) * BLOCK],
-                    tile[:, node : node + BLOCK],
-                    plain=one_plain and i == 0,
+                block = slice(i * BLOCK, (i + 1) * BLOCK)
+                nc.tensor.matmul(
+                    bank[:, block],
+                    tile[:, block],
+                    identity[:],
+                    is_transpose=not (one_plain and i == 0),
                     start=first and i == 0,
                     stop=last and i == BLOCKS - 1,
                 )
 
-        brackets = [banks.tile([BLOCK, PIECE], F32, name=f"bracket{k}", tag="bank") for k in range(PIECES)]
+        def add_onto(bank, tile, first):
+            nc.tensor.matmul(bank[:], identity[:], tile[:], start=first, stop=False)
 
+        def new_bank(name):
+            return banks.tile([BLOCK, PIECE], F32, name=name, tag="bank")
+
+        def look_up_and_multiply(b, k, factor, tag=None):
+            columns = slice(k * PIECE // 16, (k + 1) * PIECE // 16)
+            product = held_tile(f"product{b}_{k}", tag)
+            nc.vector.tensor_tensor(product[:], tables[b][:].indirect(offsets[:, columns]), factor[:], MULT)
+            return product
+
+        scalars_flipped = [held_tile(f"scalars_flipped{k}") for k in range(PIECES)]
+        for k in range(PIECES):
+            flipped_bank = new_bank("flipped_bank")
+            flip_onto(flipped_bank, scalars[k], True, True)
+            nc.scalar.activation(scalars_flipped[k][:], flipped_bank[:], COPY)
+
+        scalars_squared = [held_tile(f"scalars_squared{k}") for k in range(PIECES)]
+        for k in range(PIECES):
+            nc.scalar.activation(scalars_squared[k][:], scalars[k][:], SQUARE)
+
+        dot = [held_tile(f"dot{k}") for k in range(PIECES)]
         flipped_dot = [None] * PIECES
         upright_dot = [None] * PIECES
 
         def step_of_dot(step):
             if step < PIECES:
                 k = step
-                flipped_dot[k] = banks.tile([BLOCK, PIECE], F32, name="flipped_dot", tag="bank")
+                flipped_dot[k] = new_bank("flipped_dot")
                 squares = squared_parts.tile([FEATURES, DIMS, PIECE], F32, name="squares")
                 for d in range(DIMS):
-                    nc.scalar.activation(squares[:, d, :], vectors[:, d, piece(k)], SQUARE)
-                    flip_piece_onto(flipped_dot[k], squares[:, d, :], 0, False, d == 0, d == DIMS - 1)
+                    nc.scalar.activation(squares[:, d, :], vectors[k][:, d, :], SQUARE)
+                    flip_onto(flipped_dot[k], squares[:, d, :], d == 0, d == DIMS - 1)
             if 1 <= step <= PIECES:
                 k = step - 1
                 flipped = flipped_parts.tile([BLOCK, PIECE], F32, name="flipped", tag="flipped")
                 nc.scalar.activation(flipped[:], flipped_dot[k][:], COPY)
-                upright_dot[k] = banks.tile([FEATURES, PIECE], F32, name="upright_dot", tag="bank")
-                flip_piece_onto(upright_dot[k], flipped, 0, True, True, True)
+                upright_dot[k] = new_bank("upright_dot")
+                flip_onto(upright_dot[k], flipped, True, True, one_plain=True)
             if step >= 2:
                 k = step - 2
-                nc.scalar.activation(dot[:, piece(k)], upright_dot[k][:], COPY)
+                nc.scalar.activation(dot[k][:], upright_dot[k][:], COPY)
 
-        scalars_flipped = held.tile([BLOCK, NODES], F32, name="scalars_flipped")
-        for h in range(HALVES):
-            flipped_bank = banks.tile([BLOCK, HALF], F32, name="flipped_bank", tag="bank")
-            for column in range(0, HALF, BLOCK):
-                node = h * HALF + column
-                flip_block(
-                    flipped_bank[:, column : column + BLOCK],
-                    scalars[:, node : node + BLOCK],
-                    plain=False,
-                    start=column == 0,
-                    stop=column == HALF - BLOCK,
-                )
-            nc.scalar.activation(scalars_flipped[:, half(h)], flipped_bank[:], COPY)
-
-        for k in range(PIECES):
-            nc.scalar.activation(scalars_squared[:, piece(k)], scalars[:, piece(k)], SQUARE)
-
+        brackets = [new_bank(f"bracket{k}") for k in range(PIECES)]
+        products0 = [None] * PIECES
         lookups = [(p, k) for p in (1, 3, 0) for k in range(PIECES)]
         for step in range(PIECES + 2):
             for p, k in lookups[2 * step : 2 * step + 2]:
-                multiply(p, k)
-                if p != 0:
-                    flip_piece_onto(brackets[k], products[p], k * PIECE, p == 1, p == 1, False)
+                product = look_up_and_multiply(p, k, scalars_squared[k] if p == 3 else scalars[k])
+                if p == 0:
+                    products0[k] = product
+                else:
+                    flip_onto(brackets[k], product, p == 1, False, one_plain=p == 1)
             step_of_dot(step)
 
-        bracket_products = held.tile([BLOCK, NODES], F32, name="bracket_products")
-        contracted = held.tile([FEATURES, NODES], F32, name="contracted")
-        rests_copied = [None] * PIECES
+        contracted = [held_tile(f"contracted{k}") for k in range(PIECES)]
+        contracted_banks = [None] * PIECES
         for step in range(PIECES + 1):
             if step < PIECES:
                 k = step
-                multiply(4, k)
-                flip_piece_onto(brackets[k], products[4], k * PIECE, False, False, True)
-                multiply(2, k)
-                rest = banks.tile([BLOCK, PIECE], F32, name="rest", tag="bank")
-                flip_piece_onto(rest, products[0], k * PIECE, False, True, False)
-                flip_piece_onto(rest, products[2], k * PIECE, False, False, True)
-                rests_copied[k] = flipped_parts.tile([BLOCK, PIECE], F32, name="rest_copied", tag="flipped")
-                nc.scalar.activation(rests_copied[k][:], rest[:], COPY)
+                product = look_up_and_multiply(4, k, dot[k])
+                flip_onto(brackets[k], product, False, True)
+                product = look_up_and_multiply(2, k, dot[k], tag=f"scalars_flipped{k - 2}" if k >= 2 else None)
+                contracted_banks[k] = new_bank("contracted_bank")
+                add_onto(contracted_banks[k], products0[k], True)
+                add_onto(contracted_banks[k], product, False)
             if step >= 1:
                 k = step - 1
-                nc.vector.tensor_tensor(bracket_products[:, piece(k)], brackets[k][:], scalars_flipped[:, piece(k)], MULT)
-                contracted_bank = banks.tile([FEATURES, PIECE], F32, name="contracted_bank", tag="bank")
-                flip_piece_onto(contracted_bank, rests_copied[k], 0, False, True, False)
-                flip_piece_onto(contracted_bank, bracket_products, k * PIECE, False, False, True)
-                nc.scalar.activation(contracted[:, piece(k)], contracted_bank[:], COPY)
+                bracket_product = held_tile(f"bracket_product{k}")
+                nc.vector.tensor_tensor(bracket_product[:], brackets[k][:], scalars_flipped[k][:], MULT)
+                flip_onto(contracted_banks[k], bracket_product, False, True)
+                nc.scalar.activation(contracted[k][:], contracted_banks[k][:], COPY)
 
-        gated = held.tile([FEATURES, NODES], F32, name="gated")
         for k in range(PIECES):
+            gated = held_tile(f"gated{k}")
             width = PIECE if k < PIECES - 1 else BLOCK
-            for first_node in range(k * PIECE, (k + 1) * PIECE, width):
-                nodes = slice(first_node, first_node + width)
-                nc.vector.tensor_tensor(gated[:, nodes], looked_up(GATE, first_node, width), contracted[:, nodes], MULT)
-                nc.sync.dma_start(out[:, nodes], gated[:, nodes])
+            for first in range(0, PIECE, width):
+                part = slice(first, first + width)
+                columns = slice((k * PIECE + first) // 16, (k * PIECE + first + width) // 16)
+                nc.vector.tensor_tensor(gated[:, part], tables[GATE][:].indirect(offsets[:, columns]), contracted[k][:, part], MULT)
+                nc.sync.dma_start(out[:, k * PIECE + first : k * PIECE + first + width], gated[:, part])

@@ -85,7 +85,7 @@ def tile_equivariantproductbasisblock_kernel(tc, x0, x1, wt, offs, out):
         scalars_flipped = [held_tile(f"scalars_flipped{k}") for k in range(PIECES)]
         for k in range(PIECES):
             flipped_bank = new_bank("flipped_bank")
-            flip_onto(flipped_bank, scalars[k], True, True)
+            flip_onto(flipped_bank, scalars[k], True, True, one_plain=True)
             nc.scalar.activation(scalars_flipped[k][:], flipped_bank[:], COPY)
 
         scalars_squared = [held_tile(f"scalars_squared{k}") for k in range(PIECES)]

import concourse.mybir as mybir
from concourse.masks import make_identity

F32 = mybir.dt.float32
U16 = mybir.dt.uint16
MULT = mybir.AluOpType.mult
SQUARE = mybir.ActivationFunctionType.Square
COPY = mybir.ActivationFunctionType.Copy

FEATURES = 128
NODES = 1024
SPECIES = 256
PATHS = 5
GATE = 5
DIMS = 3
PIECE = SPECIES
PIECES = NODES // PIECE
BLOCK = 128
BLOCKS = PIECE // BLOCK


def tile_equivariantproductbasisblock_kernel(tc, x0, x1, wt, offs, out):
    nc = tc.nc

    def piece(k):
        return slice(k * PIECE, (k + 1) * PIECE)

    with (
        tc.tile_pool(name="held", bufs=1) as held,
        tc.tile_pool(name="flipped_parts", bufs=2) as flipped_parts,
        tc.tile_pool(name="squared_parts", bufs=2) as squared_parts,
        tc.psum_pool(name="banks", bufs=8) as banks,
    ):
        offsets = held.tile([FEATURES, NODES // 16], U16, name="offsets")
        nc.sync.dma_start(offsets[:], offs)

        def held_tile(name, tag=None):
            return held.tile([FEATURES, PIECE], F32, name=name, tag=tag or name)

        tables = [held.tile([FEATURES, SPECIES], F32, name=f"table{b}") for b in range(PATHS + 1)]
        scalars = [held_tile(f"scalars{k}") for k in range(PIECES)]
        vectors = [held.tile([FEATURES, DIMS, PIECE], F32, name=f"vectors{k}") for k in range(PIECES)]
        components = x1.rearrange("(d f) n -> f d n", d=DIMS)

        def load_table(queue, b):
            queue.dma_start(tables[b][:], wt[b * FEATURES : (b + 1) * FEATURES, :])

        load_table(nc.scalar, 1)
        for k in range(PIECES):
            nc.sync.dma_start(scalars[k][:], x0[:, piece(k)])
        for k in range(PIECES):
            nc.sync.dma_start(vectors[k][:], components[:, :, piece(k)])
            if k == 0:
                load_table(nc.sync, 3)
        for b in (0, 4, 2, GATE):
            load_table(nc.sync, b)

        identity = held.tile([FEATURES, FEATURES], F32, name="identity")
        make_identity(nc, identity[:])

        def flip_onto(bank, tile, first, last, one_plain=False):
            for i in range(BLOCKS):
                block = slice(i * BLOCK, (i + 1) * BLOCK)
                nc.tensor.matmul(
                    bank[:, block],
                    tile[:, block],
                    identity[:],
                    is_transpose=not (one_plain and i == 0),
                    start=first and i == 0,
                    stop=last and i == BLOCKS - 1,
                )

        def add_onto(bank, tile, first):
            nc.tensor.matmul(bank[:], identity[:], tile[:], start=first, stop=False)

        def new_bank(name):
            return banks.tile([BLOCK, PIECE], F32, name=name, tag="bank")

        def look_up_and_multiply(b, k, factor, tag=None):
            columns = slice(k * PIECE // 16, (k + 1) * PIECE // 16)
            product = held_tile(f"product{b}_{k}", tag)
            nc.vector.tensor_tensor(product[:], tables[b][:].indirect(offsets[:, columns]), factor[:], MULT)
            return product

        scalars_flipped = [held_tile(f"scalars_flipped{k}") for k in range(PIECES)]
        for k in range(PIECES):
            flipped_bank = new_bank("flipped_bank")
            flip_onto(flipped_bank, scalars[k], True, True, one_plain=True)
            nc.scalar.activation(scalars_flipped[k][:], flipped_bank[:], COPY)

        scalars_squared = [held_tile(f"scalars_squared{k}") for k in range(PIECES)]
        for k in range(PIECES):
            nc.scalar.activation(scalars_squared[k][:], scalars[k][:], SQUARE)

        dot = [held_tile(f"dot{k}") for k in range(PIECES)]
        flipped_dot = [None] * PIECES
        upright_dot = [None] * PIECES

        def step_of_dot(step):
            if step < PIECES:
                k = step
                flipped_dot[k] = new_bank("flipped_dot")
                squares = squared_parts.tile([FEATURES, DIMS, PIECE], F32, name="squares")
                for d in range(DIMS):
                    nc.scalar.activation(squares[:, d, :], vectors[k][:, d, :], SQUARE)
                    flip_onto(flipped_dot[k], squares[:, d, :], d == 0, d == DIMS - 1)
            if 1 <= step <= PIECES:
                k = step - 1
                flipped = flipped_parts.tile([BLOCK, PIECE], F32, name="flipped", tag="flipped")
                nc.scalar.activation(flipped[:], flipped_dot[k][:], COPY)
                upright_dot[k] = new_bank("upright_dot")
                flip_onto(upright_dot[k], flipped, True, True, one_plain=True)
            if step >= 2:
                k = step - 2
                nc.scalar.activation(dot[k][:], upright_dot[k][:], COPY)

        brackets = [new_bank(f"bracket{k}") for k in range(PIECES)]
        products0 = [None] * PIECES
        lookups = [(p, k) for p in (1, 3, 0) for k in range(PIECES)]
        for step in range(PIECES + 2):
            for p, k in lookups[2 * step : 2 * step + 2]:
                product = look_up_and_multiply(p, k, scalars_squared[k] if p == 3 else scalars[k])
                if p == 0:
                    products0[k] = product
                else:
                    flip_onto(brackets[k], product, p == 1, False, one_plain=p == 1)
            step_of_dot(step)

        contracted = [held_tile(f"contracted{k}") for k in range(PIECES)]
        contracted_banks = [None] * PIECES
        for step in range(PIECES + 1):
            if step < PIECES:
                k = step
                product = look_up_and_multiply(4, k, dot[k])
                flip_onto(brackets[k], product, False, True)
                product = look_up_and_multiply(2, k, dot[k], tag=f"scalars_flipped{k - 2}" if k >= 2 else None)
                contracted_banks[k] = new_bank("contracted_bank")
                add_onto(contracted_banks[k], products0[k], True)
                add_onto(contracted_banks[k], product, False)
            if step >= 1:
                k = step - 1
                bracket_product = held_tile(f"bracket_product{k}")
                nc.vector.tensor_tensor(bracket_product[:], brackets[k][:], scalars_flipped[k][:], MULT)
                flip_onto(contracted_banks[k], bracket_product, False, True)
                nc.scalar.activation(contracted[k][:], contracted_banks[k][:], COPY)

        for k in range(PIECES):
            gated = held_tile(f"gated{k}")
            width = PIECE if k < PIECES - 1 else BLOCK
            for first in range(0, PIECE, width):
                part = slice(first, first + width)
                columns = slice((k * PIECE + first) // 16, (k * PIECE + first + width) // 16)
                nc.vector.tensor_tensor(gated[:, part], tables[GATE][:].indirect(offsets[:, columns]), contracted[k][:, part], MULT)
                nc.sync.dma_start(out[:, k * PIECE + first : k * PIECE + first + width], gated[:, part])
